import numpy as np
import ml_dtypes


def mxq(x, axis, fmt="e4m3"):
    dtype, down = {"e4m3": (ml_dtypes.float8_e4m3fn, 7), "e5m2": (ml_dtypes.float8_e5m2, 14)}[fmt]
    v = np.moveaxis(np.asarray(x, np.float32).astype(ml_dtypes.bfloat16).astype(np.float64), axis, -1)
    blocks = v.reshape(v.shape[:-1] + (-1, 32))
    amax = np.abs(blocks).max(-1, keepdims=True)
    byte = np.maximum(np.where(amax > 0, np.frexp(amax)[1] - 1 + 127, 0) - down, 1)
    scale = np.exp2(byte - 127.0)
    codes = (blocks / scale).astype(np.float32).astype(dtype).astype(np.float64)
    return np.moveaxis((codes * scale).reshape(v.shape), -1, axis)


WIDE = False


def mx_kscale(k):
    if not WIDE:
        return np.ones(k)
    levels = np.array([10, -10, 5, -5, 0])
    a = np.random.permutation(np.resize(levels, k // 512 * 4)).reshape(k // 512, 4)
    idx = np.arange(k)
    return np.exp2(a[idx // 512, idx % 128 // 32])


BF16 = ml_dtypes.bfloat16


def bf(x):
    return np.asarray(x, np.float32).astype(BF16)


def f64(x):
    return np.asarray(x).astype(np.float64)


N, IN_F, OUT_F = 4096, 512, 128
POW = 2


def setup_inputs():
    s = mx_kscale(IN_F)
    u = np.exp2(np.round(np.log2(mx_kscale(N)) / 2))
    return {"input": bf(np.random.standard_normal((N, IN_F)) * s / (u * u)[:, None]),
            "adj": bf(np.random.uniform(0.0, 1.0, (N, N)) * 1.5 / N ** 0.25 * u),
            "weight": bf(np.random.uniform(-1.0, 1.0, (IN_F, OUT_F)) * 1.7 / np.sqrt(IN_F) / s[:, None]),
            "bias": bf(np.random.standard_normal(OUT_F) * 0.3)}


def reference(input, adj, weight, bias):
    k_adj = f64(adj) ** POW
    support = mxq(f64(input), 1, "e4m3") @ mxq(f64(weight), 0, "e4m3")
    out = (mxq(k_adj, 1, "e4m3") @ mxq(support, 0, "e4m3")) + f64(bias)
    return np.where(out > 0, out, np.expm1(out))

@@ -1,0 +1,326 @@
+from contextlib import ExitStack
+
+import concourse.mybir as mybir
+from concourse.masks import make_identity
+
+F32 = mybir.dt.float32
+BF16 = mybir.dt.bfloat16
+U32 = mybir.dt.uint32
+U8 = mybir.dt.uint8
+FP8X4 = mybir.dt.float8_e4m3fn_x4
+ACT = mybir.ActivationFunctionType
+ALU = mybir.AluOpType
+
+P = 128
+NODES = 4096
+IN_F = 512
+OUT_F = 128
+TILES = NODES // P
+CHUNKS = 4
+A_BUFS = 12
+FLOPS = 2 * NODES * IN_F * OUT_F + 2 * NODES * NODES * OUT_F
+
+
+def roles_of(i):
+    return "CFCF" if i % 4 == 3 else "CCCF"
+
+
+def tile_netgraphconvolution_t_kernel(tc, x, adj, weight, bias, out):
+    nc = tc.nc
+    with ExitStack() as ctx:
+        const = ctx.enter_context(tc.tile_pool(name="const", bufs=1))
+        a_pool = ctx.enter_context(tc.tile_pool(name="a_pool", bufs=A_BUFS))
+        raw_pool = ctx.enter_context(tc.tile_pool(name="raw_pool", bufs=3))
+        grp_pool = ctx.enter_context(tc.tile_pool(name="grp_pool", bufs=3))
+        q_pool = ctx.enter_context(tc.tile_pool(name="q_pool", bufs=4))
+        ep_pool = ctx.enter_context(tc.tile_pool(name="ep_pool", bufs=2))
+        tp_pool = ctx.enter_context(tc.psum_pool(name="tp_pool", bufs=6))
+        acc_pool = ctx.enter_context(tc.psum_pool(name="acc_pool", bufs=2))
+        ctx.enter_context(tc.manual_schedule())
+
+        x_view = x.rearrange("(n p e) k -> p n (e k)", n=16, p=P, e=2)
+        w_view = weight.rearrange("(u q e) c -> q u (e c)", u=2, q=P, e=2)
+        adj_view = adj.rearrange("(g p s) k -> g s p k", g=8, p=P, s=4)
+        out_view = out.rearrange("(g p s) f -> g p s f", g=8, p=P, s=4)
+
+        ident = const.tile([P, P], F32, name="ident")
+        make_identity(nc, ident[:])
+
+        warm = const.tile([P, 2], F32, name="warm")
+        nc.vector.memset(warm[:, 0:1], 0.0)
+        nc.scalar.activation(out=warm[:, 1:2], in_=warm[:, 0:1], func=ACT.Exp)
+
+        a_tiles = {}
+
+        def load_x(h):
+            t = a_pool.tile([P, 4096], BF16, name="a", tag="a")
+            nc.sync.dma_start(
+                out=t[:].rearrange("p (n k) -> p n k", n=4),
+                in_=x_view[:, 4 * h : 4 * h + 4, :],
+            )
+            a_tiles[("x", h)] = t
+
+        def load_a(i):
+            if i >= TILES:
+                return
+            t = a_pool.tile([P, 4096], BF16, name="a", tag="a")
+            nc.sync.dma_start(out=t[:], in_=adj_view[i // 4, i % 4])
+            a_tiles[("a", i)] = t
+
+        banks = {}
+
+        def transposes(key):
+            words = a_tiles[key][:].bitcast(F32)
+            made = []
+            for b in range(4):
+                tp = tp_pool.tile([P, 2, 256], F32, name="tp", tag="tp")
+                for g in range(2):
+                    for u in range(2):
+                        col = 512 * b + 256 * g + 128 * u
+                        nc.tensor.transpose(
+                            tp[:, u, 128 * g : 128 * g + 128],
+                            words[:, col : col + 128],
+                            ident[:],
+                        )
+                made.append(tp)
+            banks[key] = made
+
+        def new_codes():
+            codes = q_pool.tile([P, 1024], U32, name="codes", tag="codes", align_bytes=64)
+            scales = q_pool.tile([P, 1024], U8, name="scales", tag="scales", align_bytes=64)
+            return codes, scales
+
+        def quantise(grp, codes, scales, lo, hi):
+            nc.vector.quantize_mx(
+                out=codes[:, lo // 4 : hi // 4].bitcast(FP8X4),
+                scales=scales[:, lo // 4 : hi // 4],
+                in_=grp[:, lo:hi],
+            )
+
+        def words_out(engine_copy, dst_f32, tp, b):
+            engine_copy(
+                out=dst_f32[:, 512 * b : 512 * b + 512].rearrange("p (c u) -> p c u", u=2),
+                in_=tp[:].rearrange("p u c -> p c u"),
+            )
+
+        w_raw = const.tile([P, 4, OUT_F], BF16, name="w_raw")
+        nc.sync.dma_start(out=w_raw[:].rearrange("p (u e) c -> p u (e c)", u=2), in_=w_view)
+        for h in range(CHUNKS):
+            load_x(h)
+        for i in range(A_BUFS - CHUNKS):
+            load_a(i)
+
+        w_grp = const.tile([P, OUT_F, 4], BF16, name="w_grp", align_bytes=64)
+        w_codes = const.tile([P, OUT_F], U32, name="w_codes", align_bytes=64)
+        w_scales = const.tile([P, OUT_F], U8, name="w_scales", align_bytes=64)
+        nc.vector.tensor_copy(out=w_grp[:], in_=w_raw[:].rearrange("p t c -> p c t"))
+        nc.vector.quantize_mx(
+            out=w_codes[:].bitcast(FP8X4),
+            scales=w_scales[:],
+            in_=w_grp[:].rearrange("p c t -> p (c t)"),
+        )
+
+        sup_grp = const.tile([P, 8, OUT_F, 4], BF16, name="sup_grp", align_bytes=64)
+        sup_codes = const.tile([P, 1024], U32, name="sup_codes", align_bytes=64)
+        sup_scales = const.tile([P, 1024], U8, name="sup_scales", align_bytes=64)
+        x_grp = {}
+        x_q = {}
+        x_acc = {}
+
+        def x_out(h):
+            grp = grp_pool.tile([P, 4096], BF16, name="grp", tag="grp", align_bytes=64)
+            x_grp[h] = grp
+            dst = grp[:].bitcast(F32)
+            made = banks[("x", h)]
+            for b in range(3):
+                words_out(nc.scalar.copy, dst, made[b], b)
+            words_out(nc.vector.tensor_copy, dst, made[3], 3)
+
+        def x_quant(h):
+            x_q[h] = new_codes()
+            quantise(x_grp[h], x_q[h][0], x_q[h][1], 0, 4096)
+
+        def x_matmuls(h):
+            codes, scales = x_q[h]
+            made = []
+            for cc in range(2):
+                acc = acc_pool.tile([P, 4, OUT_F], F32, name="acc", tag="acc")
+                for t in range(4):
+                    col = 512 * cc + 128 * t
+                    nc.tensor.matmul_mx(
+                        out=acc[:, t, :],
+                        lhsT=codes[:, col : col + 128].bitcast(FP8X4),
+                        lhsT_scale=scales[:, col : col + 128],
+                        rhs=w_codes[:].bitcast(FP8X4),
+                        rhs_scale=w_scales[:],
+                        start=True,
+                        stop=True,
+                    )
+                made.append(acc)
+            x_acc[h] = made
+
+        def sup_out(h):
+            nc.scalar.copy(
+                out=sup_grp[:, 2 * h, :, :], in_=x_acc[h][0][:].rearrange("p t w -> p w t")
+            )
+            nc.vector.tensor_copy(
+                out=sup_grp[:, 2 * h + 1, :, :], in_=x_acc[h][1][:].rearrange("p t w -> p w t")
+            )
+
+        a_grp = {}
+        a_q = {}
+
+        def a_out(i):
+            roles = roles_of(i)
+            grp = grp_pool.tile([P, 4096], BF16, name="grp", tag="grp", align_bytes=64)
+            raw = raw_pool.tile([P, 2048], F32, name="raw", tag="raw")
+            a_grp[i] = (grp, raw)
+            made = banks[("a", i)]
+            for b in range(4):
+                if roles[b] == "C":
+                    words_out(nc.scalar.copy, raw, made[b], b)
+                else:
+                    nc.scalar.activation(
+                        out=grp[:, 1024 * b : 1024 * b + 1024].rearrange(
+                            "p (c u e) -> p c u e", u=2, e=2
+                        ),
+                        in_=made[b][:].bitcast(BF16).rearrange("p u (c e) -> p c u e", e=2),
+                        func=ACT.Square,
+                    )
+
+        def a_quant(i):
+            roles = roles_of(i)
+            grp, raw = a_grp[i]
+            raw_bf = raw[:].bitcast(BF16)
+            for half in range(2):
+                todo = [b for b in (2 * half, 2 * half + 1) if roles[b] == "C"]
+                if len(todo) > 0:
+                    lo = 1024 * todo[0]
+                    hi = 1024 * todo[-1] + 1024
+                    nc.vector.tensor_tensor(
+                        out=grp[:, lo:hi], in0=raw_bf[:, lo:hi], in1=raw_bf[:, lo:hi], op=ALU.mult
+                    )
+            a_q[i] = new_codes()
+            quantise(grp, a_q[i][0], a_q[i][1], 0, 2048)
+            quantise(grp, a_q[i][0], a_q[i][1], 2048, 4096)
+
+        units = [[4 * g, 4 * g + 1, 4 * g + 2, 4 * g + 3] for g in range(7)] + [[28, 29, 30], [31]]
+        unit_of = {}
+        for n, rows in enumerate(units):
+            for i in rows:
+                unit_of[i] = n
+        unit_acc = {}
+        unit_ep = {}
+
+        def a_matmuls(i):
+            n = unit_of[i]
+            if i == units[n][0]:
+                unit_acc[n] = acc_pool.tile([P, 4, OUT_F], F32, name="acc", tag="acc")
+            acc = unit_acc[n]
+            codes, scales = a_q[i]
+            s = i - units[n][0]
+            for g in range(8):
+                cols = slice(128 * g, 128 * g + 128)
+                nc.tensor.matmul_mx(
+                    out=acc[:, s, :],
+                    lhsT=codes[:, cols].bitcast(FP8X4),
+                    lhsT_scale=scales[:, cols],
+                    rhs=sup_codes[:, cols].bitcast(FP8X4),
+                    rhs_scale=sup_scales[:, cols],
+                    start=(g == 0),
+                    stop=(g == 7),
+                )
+
+        bias_bf = const.tile([P, OUT_F], BF16, name="bias_bf")
+        bias_f = const.tile([P, OUT_F], F32, name="bias_f")
+
+        def ep_first(n):
+            k = len(units[n])
+            v = ep_pool.tile([P, 4, OUT_F], F32, name="v", tag="v")
+            m = ep_pool.tile([P, 4, OUT_F], F32, name="m", tag="m")
+            nc.vector.tensor_tensor(
+                out=v[:, 0:k, :],
+                in0=unit_acc[n][:, 0:k, :],
+                in1=bias_f[:].unsqueeze(1).to_broadcast([P, k, OUT_F]),
+                op=ALU.add,
+            )
+            nc.vector.tensor_scalar_min(out=m[:, 0:k, :], in0=v[:, 0:k, :], scalar1=0.0)
+            unit_ep[n] = (v, m)
+
+        def ep_exp(n):
+            k = len(units[n])
+            v, m = unit_ep[n]
+            e = ep_pool.tile([P, 4, OUT_F], F32, name="e", tag="e")
+            nc.scalar.activation(out=e[:, 0:k, :], in_=m[:, 0:k, :], func=ACT.Exp)
+            unit_ep[n] = (v, e)
+
+        def ep_last(n):
+            k = len(units[n])
+            v, e = unit_ep[n]
+            o = ep_pool.tile([P, 4, OUT_F], F32, name="o", tag="o")
+            nc.vector.scalar_tensor_tensor(
+                out=o[:, 0:k, :],
+                in0=e[:, 0:k, :],
+                scalar=-1.0,
+                in1=v[:, 0:k, :],
+                op0=ALU.add,
+                op1=ALU.max,
+            )
+            first = units[n][0]
+            s0 = first % 4
+            nc.sync.dma_start(out=out_view[first // 4][:, s0 : s0 + k, :], in_=o[:, 0:k, :])
+
+        transposes(("x", 0))
+        for h in range(CHUNKS):
+            load_a(A_BUFS - CHUNKS + h)
+            if h + 1 < CHUNKS:
+                transposes(("x", h + 1))
+            else:
+                transposes(("a", 0))
+                load_a(A_BUFS)
+            x_out(h)
+            if h > 0:
+                sup_out(h - 1)
+            x_quant(h)
+            x_matmuls(h)
+        transposes(("a", 1))
+        load_a(A_BUFS + 1)
+
+        steps = {}
+
+        def later(i, what, n):
+            steps[i] = steps.get(i, []) + [(what, n)]
+
+        for n, rows in enumerate(units):
+            later(rows[-1] + 1, "first", n)
+            later(rows[-1] + 2, "rest", n)
+
+        for i in range(TILES + 3):
+            if i + 2 < TILES:
+                transposes(("a", i + 2))
+                load_a(i + 2 + A_BUFS)
+            if i < TILES:
+                a_out(i)
+            for what, n in steps.get(i, []):
+                if what == "rest":
+                    ep_exp(n)
+            if i < TILES:
+                a_quant(i)
+            if i == 0:
+                sup_out(CHUNKS - 1)
+                nc.vector.quantize_mx(
+                    out=sup_codes[:].bitcast(FP8X4),
+                    scales=sup_scales[:],
+                    in_=sup_grp[:].rearrange("p c w t -> p (c w t)"),
+                )
+            if i == 1:
+                nc.sync.dma_start(out=bias_bf[:], in_=bias.partition_broadcast(P))
+            if i == 3:
+                nc.vector.tensor_copy(out=bias_f[:], in_=bias_bf[:])
+            if i < TILES:
+                a_matmuls(i)
+            for what, n in steps.get(i, []):
+                if what == "first":
+                    ep_first(n)
+                else:
+                    ep_last(n)

@@ -18,11 +18,15 @@ OUT_F = 128
 TILES = NODES // P
 CHUNKS = 4
 A_BUFS = 12
+X_PIECES = (4, 2, 1, 1)
 FLOPS = 2 * NODES * IN_F * OUT_F + 2 * NODES * NODES * OUT_F
 
 
-def roles_of(i):
-    return "CFCF" if i % 4 == 3 else "CCCF"
+TWO_COPIES = (3, 7, 11, 15, 19, 23, 27, 29, 30, 31)
+
+
+def copies_of(i):
+    return 2 if i in TWO_COPIES else 3
 
 
 def tile_netgraphconvolution_t_kernel(tc, x, adj, weight, bias, out):
@@ -31,7 +35,7 @@ def tile_netgraphconvolution_t_kernel(tc, x, adj, weight, bias, out):
         const = ctx.enter_context(tc.tile_pool(name="const", bufs=1))
         a_pool = ctx.enter_context(tc.tile_pool(name="a_pool", bufs=A_BUFS))
         raw_pool = ctx.enter_context(tc.tile_pool(name="raw_pool", bufs=3))
-        grp_pool = ctx.enter_context(tc.tile_pool(name="grp_pool", bufs=3))
+        grp_pool = ctx.enter_context(tc.tile_pool(name="grp_pool", bufs=4))
         q_pool = ctx.enter_context(tc.tile_pool(name="q_pool", bufs=4))
         ep_pool = ctx.enter_context(tc.tile_pool(name="ep_pool", bufs=2))
         tp_pool = ctx.enter_context(tc.psum_pool(name="tp_pool", bufs=6))
@@ -54,10 +58,15 @@ def tile_netgraphconvolution_t_kernel(tc, x, adj, weight, bias, out):
 
         def load_x(h):
             t = a_pool.tile([P, 4096], BF16, name="a", tag="a")
-            nc.sync.dma_start(
-                out=t[:].rearrange("p (n k) -> p n k", n=4),
-                in_=x_view[:, 4 * h : 4 * h + 4, :],
-            )
+            pieces = X_PIECES[h]
+            step = 4 // pieces
+            for j in range(pieces):
+                nc.sync.dma_start(
+                    out=t[:, 1024 * step * j : 1024 * step * (j + 1)].rearrange(
+                        "p (n k) -> p n k", n=step
+                    ),
+                    in_=x_view[:, 4 * h + step * j : 4 * h + step * (j + 1), :],
+                )
             a_tiles[("x", h)] = t
 
         def load_a(i):
@@ -104,11 +113,15 @@ def tile_netgraphconvolution_t_kernel(tc, x, adj, weight, bias, out):
             )
 
         w_raw = const.tile([P, 4, OUT_F], BF16, name="w_raw")
-        nc.sync.dma_start(out=w_raw[:].rearrange("p (u e) c -> p u (e c)", u=2), in_=w_view)
         for h in range(CHUNKS):
             load_x(h)
+            if h == 0:
+                nc.sync.dma_start(out=w_raw[:].rearrange("p (u e) c -> p u (e c)", u=2), in_=w_view)
+        bias_bf = const.tile([P, OUT_F], BF16, name="bias_bf")
         for i in range(A_BUFS - CHUNKS):
             load_a(i)
+            if i == 1:
+                nc.sync.dma_start(out=bias_bf[:], in_=bias.partition_broadcast(P))
 
         w_grp = const.tile([P, OUT_F, 4], BF16, name="w_grp", align_bytes=64)
         w_codes = const.tile([P, OUT_F], U32, name="w_codes", align_bytes=64)
@@ -171,13 +184,12 @@ def tile_netgraphconvolution_t_kernel(tc, x, adj, weight, bias, out):
         a_q = {}
 
         def a_out(i):
-            roles = roles_of(i)
             grp = grp_pool.tile([P, 4096], BF16, name="grp", tag="grp", align_bytes=64)
             raw = raw_pool.tile([P, 2048], F32, name="raw", tag="raw")
             a_grp[i] = (grp, raw)
             made = banks[("a", i)]
             for b in range(4):
-                if roles[b] == "C":
+                if b < copies_of(i):
                     words_out(nc.scalar.copy, raw, made[b], b)
                 else:
                     nc.scalar.activation(
@@ -188,21 +200,17 @@ def tile_netgraphconvolution_t_kernel(tc, x, adj, weight, bias, out):
                         func=ACT.Square,
                     )
 
-        def a_quant(i):
-            roles = roles_of(i)
+        def a_square(i):
             grp, raw = a_grp[i]
             raw_bf = raw[:].bitcast(BF16)
-            for half in range(2):
-                todo = [b for b in (2 * half, 2 * half + 1) if roles[b] == "C"]
-                if len(todo) > 0:
-                    lo = 1024 * todo[0]
-                    hi = 1024 * todo[-1] + 1024
-                    nc.vector.tensor_tensor(
-                        out=grp[:, lo:hi], in0=raw_bf[:, lo:hi], in1=raw_bf[:, lo:hi], op=ALU.mult
-                    )
+            hi = 1024 * copies_of(i)
+            nc.vector.tensor_tensor(
+                out=grp[:, 0:hi], in0=raw_bf[:, 0:hi], in1=raw_bf[:, 0:hi], op=ALU.mult
+            )
+
+        def a_quant(i):
             a_q[i] = new_codes()
-            quantise(grp, a_q[i][0], a_q[i][1], 0, 2048)
-            quantise(grp, a_q[i][0], a_q[i][1], 2048, 4096)
+            quantise(a_grp[i][0], a_q[i][0], a_q[i][1], 0, 4096)
 
         units = [[4 * g, 4 * g + 1, 4 * g + 2, 4 * g + 3] for g in range(7)] + [[28, 29, 30], [31]]
         unit_of = {}
@@ -231,7 +239,6 @@ def tile_netgraphconvolution_t_kernel(tc, x, adj, weight, bias, out):
                     stop=(g == 7),
                 )
 
-        bias_bf = const.tile([P, OUT_F], BF16, name="bias_bf")
         bias_f = const.tile([P, OUT_F], F32, name="bias_f")
 
         def ep_first(n):
@@ -286,26 +293,22 @@ def tile_netgraphconvolution_t_kernel(tc, x, adj, weight, bias, out):
         transposes(("a", 1))
         load_a(A_BUFS + 1)
 
-        steps = {}
+        first_at = {}
+        exp_at = {}
+        last_at = {}
+        for n, rows in enumerate(units[:-2]):
+            first_at[rows[-1] + 2] = n
+            exp_at[rows[-1] + 3] = n
+            last_at[rows[-1] + 3] = n
 
-        def later(i, what, n):
-            steps[i] = steps.get(i, []) + [(what, n)]
-
-        for n, rows in enumerate(units):
-            later(rows[-1] + 1, "first", n)
-            later(rows[-1] + 2, "rest", n)
-
-        for i in range(TILES + 3):
+        for i in range(TILES - 1):
             if i + 2 < TILES:
                 transposes(("a", i + 2))
                 load_a(i + 2 + A_BUFS)
-            if i < TILES:
-                a_out(i)
-            for what, n in steps.get(i, []):
-                if what == "rest":
-                    ep_exp(n)
-            if i < TILES:
-                a_quant(i)
+            a_out(i)
+            if i in exp_at:
+                ep_exp(exp_at[i])
+            a_square(i)
             if i == 0:
                 sup_out(CHUNKS - 1)
                 nc.vector.quantize_mx(
@@ -313,14 +316,26 @@ def tile_netgraphconvolution_t_kernel(tc, x, adj, weight, bias, out):
                     scales=sup_scales[:],
                     in_=sup_grp[:].rearrange("p c w t -> p (c w t)"),
                 )
-            if i == 1:
-                nc.sync.dma_start(out=bias_bf[:], in_=bias.partition_broadcast(P))
             if i == 3:
                 nc.vector.tensor_copy(out=bias_f[:], in_=bias_bf[:])
-            if i < TILES:
-                a_matmuls(i)
-            for what, n in steps.get(i, []):
-                if what == "first":
-                    ep_first(n)
-                else:
-                    ep_last(n)
+            if i >= 1:
+                a_quant(i - 1)
+                a_matmuls(i - 1)
+            if i in first_at:
+                ep_first(first_at[i])
+            if i in last_at:
+                ep_last(last_at[i])
+
+        last = TILES - 1
+        a_out(last)
+        a_quant(last - 1)
+        a_matmuls(last - 1)
+        a_square(last)
+        ep_first(len(units) - 2)
+        ep_exp(len(units) - 2)
+        a_quant(last)
+        a_matmuls(last)
+        ep_last(len(units) - 2)
+        ep_first(len(units) - 1)
+        ep_exp(len(units) - 1)
+        ep_last(len(units) - 1)

@@ -19,14 +19,16 @@ TILES = NODES // P
 CHUNKS = 4
 A_BUFS = 12
 X_PIECES = (4, 2, 1, 1)
+END_CUTS = (0, 2048, 3072, 4096)
 FLOPS = 2 * NODES * IN_F * OUT_F + 2 * NODES * NODES * OUT_F
 
 
-TWO_COPIES = (3, 7, 11, 15, 19, 23, 27, 29, 30, 31)
+COPIES = (3, 3, 3, 3, 3, 3, 3, 3, 3, 3, 3, 2, 3, 3, 3, 3, 3, 3, 3, 2, 3, 3, 3, 3, 3, 3, 3, 2, 3, 3, 3, 2)
+JOBS = (("x", 0), ("x", 1), ("x", 2), ("x", 3))
 
 
 def copies_of(i):
-    return 2 if i in TWO_COPIES else 3
+    return COPIES[i]
 
 
 def tile_netgraphconvolution_t_kernel(tc, x, adj, weight, bias, out):
@@ -204,13 +206,15 @@ def tile_netgraphconvolution_t_kernel(tc, x, adj, weight, bias, out):
             grp, raw = a_grp[i]
             raw_bf = raw[:].bitcast(BF16)
             hi = 1024 * copies_of(i)
-            nc.vector.tensor_tensor(
-                out=grp[:, 0:hi], in0=raw_bf[:, 0:hi], in1=raw_bf[:, 0:hi], op=ALU.mult
-            )
+            if hi > 0:
+                nc.vector.tensor_tensor(
+                    out=grp[:, 0:hi], in0=raw_bf[:, 0:hi], in1=raw_bf[:, 0:hi], op=ALU.mult
+                )
 
-        def a_quant(i):
-            a_q[i] = new_codes()
-            quantise(a_grp[i][0], a_q[i][0], a_q[i][1], 0, 4096)
+        def a_quant(i, lo=0, hi=4096):
+            if lo == 0:
+                a_q[i] = new_codes()
+            quantise(a_grp[i][0], a_q[i][0], a_q[i][1], lo, hi)
 
         units = [[4 * g, 4 * g + 1, 4 * g + 2, 4 * g + 3] for g in range(7)] + [[28, 29, 30], [31]]
         unit_of = {}
@@ -220,14 +224,14 @@ def tile_netgraphconvolution_t_kernel(tc, x, adj, weight, bias, out):
         unit_acc = {}
         unit_ep = {}
 
-        def a_matmuls(i):
+        def a_matmuls(i, g_lo=0, g_hi=8):
             n = unit_of[i]
-            if i == units[n][0]:
+            if i == units[n][0] and g_lo == 0:
                 unit_acc[n] = acc_pool.tile([P, 4, OUT_F], F32, name="acc", tag="acc")
             acc = unit_acc[n]
             codes, scales = a_q[i]
             s = i - units[n][0]
-            for g in range(8):
+            for g in range(g_lo, g_hi):
                 cols = slice(128 * g, 128 * g + 128)
                 nc.tensor.matmul_mx(
                     out=acc[:, s, :],
@@ -333,9 +337,12 @@ def tile_netgraphconvolution_t_kernel(tc, x, adj, weight, bias, out):
         a_square(last)
         ep_first(len(units) - 2)
         ep_exp(len(units) - 2)
-        a_quant(last)
-        a_matmuls(last)
-        ep_last(len(units) - 2)
+        cuts = END_CUTS
+        for c in range(len(cuts) - 1):
+            a_quant(last, cuts[c], cuts[c + 1])
+            a_matmuls(last, cuts[c] // 512, cuts[c + 1] // 512)
+            if c == 0:
+                ep_last(len(units) - 2)
         ep_first(len(units) - 1)
         ep_exp(len(units) - 1)
         ep_last(len(units) - 1)

@@ -23,7 +23,7 @@ END_CUTS = (0, 2048, 3072, 4096)
 FLOPS = 2 * NODES * IN_F * OUT_F + 2 * NODES * NODES * OUT_F
 
 
-COPIES = (3, 3, 3, 3, 3, 3, 3, 3, 3, 3, 3, 2, 3, 3, 3, 3, 3, 3, 3, 2, 3, 3, 3, 3, 3, 3, 3, 2, 3, 3, 3, 2)
+COPIES = (3, 2, 3, 2, 3, 2, 3, 2, 3, 2, 3, 2, 3, 2, 3, 2, 3, 2, 3, 2, 3, 2, 3, 2, 3, 2, 3, 2, 2, 2, 2, 2)
 JOBS = (("x", 0), ("x", 1), ("x", 2), ("x", 3))
 
 

@@ -38,7 +38,7 @@ def tile_netgraphconvolution_t_kernel(tc, x, adj, weight, bias, out):
         a_pool = ctx.enter_context(tc.tile_pool(name="a_pool", bufs=A_BUFS))
         raw_pool = ctx.enter_context(tc.tile_pool(name="raw_pool", bufs=3))
         grp_pool = ctx.enter_context(tc.tile_pool(name="grp_pool", bufs=4))
-        q_pool = ctx.enter_context(tc.tile_pool(name="q_pool", bufs=4))
+        q_pool = ctx.enter_context(tc.tile_pool(name="q_pool", bufs=5))
         ep_pool = ctx.enter_context(tc.tile_pool(name="ep_pool", bufs=2))
         tp_pool = ctx.enter_context(tc.psum_pool(name="tp_pool", bufs=6))
         acc_pool = ctx.enter_context(tc.psum_pool(name="acc_pool", bufs=2))
@@ -298,20 +298,24 @@ def tile_netgraphconvolution_t_kernel(tc, x, adj, weight, bias, out):
         load_a(A_BUFS + 1)
 
         first_at = {}
-        exp_at = {}
-        last_at = {}
-        for n, rows in enumerate(units[:-2]):
-            first_at[rows[-1] + 2] = n
-            exp_at[rows[-1] + 3] = n
-            last_at[rows[-1] + 3] = n
+        rest_at = {}
+
+        def multiply(i, at):
+            a_matmuls(i)
+            n = unit_of[i]
+            if i == units[n][-1] and n < len(units) - 2:
+                first_at[at + 2] = n
+                rest_at[at + 3] = n
 
         for i in range(TILES - 1):
-            if i + 2 < TILES:
-                transposes(("a", i + 2))
-                load_a(i + 2 + A_BUFS)
+            if i % 2 == 0:
+                for k in (i + 2, i + 3):
+                    if 2 <= k < TILES:
+                        transposes(("a", k))
+                        load_a(k + A_BUFS)
             a_out(i)
-            if i in exp_at:
-                ep_exp(exp_at[i])
+            if i in rest_at:
+                ep_exp(rest_at[i])
             a_square(i)
             if i == 0:
                 sup_out(CHUNKS - 1)
@@ -324,17 +328,25 @@ def tile_netgraphconvolution_t_kernel(tc, x, adj, weight, bias, out):
                 nc.vector.tensor_copy(out=bias_f[:], in_=bias_bf[:])
             if i >= 1:
                 a_quant(i - 1)
-                a_matmuls(i - 1)
+            if i % 2 == 0 and i >= 2:
+                multiply(i - 2, i)
+                multiply(i - 1, i)
             if i in first_at:
                 ep_first(first_at[i])
-            if i in last_at:
-                ep_last(last_at[i])
+            if i in rest_at:
+                ep_last(rest_at[i])
 
+        assert all([k < TILES - 1 for k in first_at])
         last = TILES - 1
         a_out(last)
+        late = [rest_at[k] for k in sorted(rest_at) if k >= last]
+        for n in late:
+            ep_exp(n)
         a_quant(last - 1)
         a_matmuls(last - 1)
         a_square(last)
+        for n in late:
+            ep_last(n)
         ep_first(len(units) - 2)
         ep_exp(len(units) - 2)
         cuts = END_CUTS

from contextlib import ExitStack

import concourse.mybir as mybir
from concourse.masks import make_identity

F32 = mybir.dt.float32
BF16 = mybir.dt.bfloat16
U32 = mybir.dt.uint32
U8 = mybir.dt.uint8
FP8X4 = mybir.dt.float8_e4m3fn_x4
ACT = mybir.ActivationFunctionType
ALU = mybir.AluOpType

P = 128
NODES = 4096
IN_F = 512
OUT_F = 128
TILES = NODES // P
CHUNKS = 4
A_BUFS = 12
X_PIECES = (4, 2, 1, 1)
END_CUTS = (0, 2048, 3072, 4096)
FLOPS = 2 * NODES * IN_F * OUT_F + 2 * NODES * NODES * OUT_F


COPIES = (3, 2, 3, 2, 3, 2, 3, 2, 3, 2, 3, 2, 3, 2, 3, 2, 3, 2, 3, 2, 3, 2, 3, 2, 3, 2, 3, 2, 2, 2, 2, 2)
JOBS = (("x", 0), ("x", 1), ("x", 2), ("x", 3))


def copies_of(i):
    return COPIES[i]


def tile_netgraphconvolution_t_kernel(tc, x, adj, weight, bias, out):
    nc = tc.nc
    with ExitStack() as ctx:
        const = ctx.enter_context(tc.tile_pool(name="const", bufs=1))
        a_pool = ctx.enter_context(tc.tile_pool(name="a_pool", bufs=A_BUFS))
        raw_pool = ctx.enter_context(tc.tile_pool(name="raw_pool", bufs=3))
        grp_pool = ctx.enter_context(tc.tile_pool(name="grp_pool", bufs=4))
        q_pool = ctx.enter_context(tc.tile_pool(name="q_pool", bufs=5))
        ep_pool = ctx.enter_context(tc.tile_pool(name="ep_pool", bufs=2))
        tp_pool = ctx.enter_context(tc.psum_pool(name="tp_pool", bufs=6))
        acc_pool = ctx.enter_context(tc.psum_pool(name="acc_pool", bufs=2))
        ctx.enter_context(tc.manual_schedule())

        x_view = x.rearrange("(n p e) k -> p n (e k)", n=16, p=P, e=2)
        w_view = weight.rearrange("(u q e) c -> q u (e c)", u=2, q=P, e=2)
        adj_view = adj.rearrange("(g p s) k -> g s p k", g=8, p=P, s=4)
        out_view = out.rearrange("(g p s) f -> g p s f", g=8, p=P, s=4)

        ident = const.tile([P, P], F32, name="ident")
        make_identity(nc, ident[:])

        warm = const.tile([P, 2], F32, name="warm")
        nc.vector.memset(warm[:, 0:1], 0.0)
        nc.scalar.activation(out=warm[:, 1:2], in_=warm[:, 0:1], func=ACT.Exp)

        a_tiles = {}

        def load_x(h):
            t = a_pool.tile([P, 4096], BF16, name="a", tag="a")
            pieces = X_PIECES[h]
            step = 4 // pieces
            for j in range(pieces):
                nc.sync.dma_start(
                    out=t[:, 1024 * step * j : 1024 * step * (j + 1)].rearrange(
                        "p (n k) -> p n k", n=step
                    ),
                    in_=x_view[:, 4 * h + step * j : 4 * h + step * (j + 1), :],
                )
            a_tiles[("x", h)] = t

        def load_a(i):
            if i >= TILES:
                return
            t = a_pool.tile([P, 4096], BF16, name="a", tag="a")
            nc.sync.dma_start(out=t[:], in_=adj_view[i // 4, i % 4])
            a_tiles[("a", i)] = t

        banks = {}

        def transposes(key):
            words = a_tiles[key][:].bitcast(F32)
            made = []
            for b in range(4):
                tp = tp_pool.tile([P, 2, 256], F32, name="tp", tag="tp")
                for g in range(2):
                    for u in range(2):
                        col = 512 * b + 256 * g + 128 * u
                        nc.tensor.transpose(
                            tp[:, u, 128 * g : 128 * g + 128],
                            words[:, col : col + 128],
                            ident[:],
                        )
                made.append(tp)
            banks[key] = made

        def new_codes():
            codes = q_pool.tile([P, 1024], U32, name="codes", tag="codes", align_bytes=64)
            scales = q_pool.tile([P, 1024], U8, name="scales", tag="scales", align_bytes=64)
            return codes, scales

        def quantise(grp, codes, scales, lo, hi):
            nc.vector.quantize_mx(
                out=codes[:, lo // 4 : hi // 4].bitcast(FP8X4),
                scales=scales[:, lo // 4 : hi // 4],
                in_=grp[:, lo:hi],
            )

        def words_out(engine_copy, dst_f32, tp, b):
            engine_copy(
                out=dst_f32[:, 512 * b : 512 * b + 512].rearrange("p (c u) -> p c u", u=2),
                in_=tp[:].rearrange("p u c -> p c u"),
            )

        w_raw = const.tile([P, 4, OUT_F], BF16, name="w_raw")
        for h in range(CHUNKS):
            load_x(h)
            if h == 0:
                nc.sync.dma_start(out=w_raw[:].rearrange("p (u e) c -> p u (e c)", u=2), in_=w_view)
        bias_bf = const.tile([P, OUT_F], BF16, name="bias_bf")
        for i in range(A_BUFS - CHUNKS):
            load_a(i)
            if i == 1:
                nc.sync.dma_start(out=bias_bf[:], in_=bias.partition_broadcast(P))

        w_grp = const.tile([P, OUT_F, 4], BF16, name="w_grp", align_bytes=64)
        w_codes = const.tile([P, OUT_F], U32, name="w_codes", align_bytes=64)
        w_scales = const.tile([P, OUT_F], U8, name="w_scales", align_bytes=64)
        nc.vector.tensor_copy(out=w_grp[:], in_=w_raw[:].rearrange("p t c -> p c t"))
        nc.vector.quantize_mx(
            out=w_codes[:].bitcast(FP8X4),
            scales=w_scales[:],
            in_=w_grp[:].rearrange("p c t -> p (c t)"),
        )

        sup_grp = const.tile([P, 8, OUT_F, 4], BF16, name="sup_grp", align_bytes=64)
        sup_codes = const.tile([P, 1024], U32, name="sup_codes", align_bytes=64)
        sup_scales = const.tile([P, 1024], U8, name="sup_scales", align_bytes=64)
        x_grp = {}
        x_q = {}
        x_acc = {}

        def x_out(h):
            grp = grp_pool.tile([P, 4096], BF16, name="grp", tag="grp", align_bytes=64)
            x_grp[h] = grp
            dst = grp[:].bitcast(F32)
            made = banks[("x", h)]
            for b in range(3):
                words_out(nc.scalar.copy, dst, made[b], b)
            words_out(nc.vector.tensor_copy, dst, made[3], 3)

        def x_quant(h):
            x_q[h] = new_codes()
            quantise(x_grp[h], x_q[h][0], x_q[h][1], 0, 4096)

        def x_matmuls(h):
            codes, scales = x_q[h]
            made = []
            for cc in range(2):
                acc = acc_pool.tile([P, 4, OUT_F], F32, name="acc", tag="acc")
                for t in range(4):
                    col = 512 * cc + 128 * t
                    nc.tensor.matmul_mx(
                        out=acc[:, t, :],
                        lhsT=codes[:, col : col + 128].bitcast(FP8X4),
                        lhsT_scale=scales[:, col : col + 128],
                        rhs=w_codes[:].bitcast(FP8X4),
                        rhs_scale=w_scales[:],
                        start=True,
                        stop=True,
                    )
                made.append(acc)
            x_acc[h] = made

        def sup_out(h):
            nc.scalar.copy(
                out=sup_grp[:, 2 * h, :, :], in_=x_acc[h][0][:].rearrange("p t w -> p w t")
            )
            nc.vector.tensor_copy(
                out=sup_grp[:, 2 * h + 1, :, :], in_=x_acc[h][1][:].rearrange("p t w -> p w t")
            )

        a_grp = {}
        a_q = {}

        def a_out(i):
            grp = grp_pool.tile([P, 4096], BF16, name="grp", tag="grp", align_bytes=64)
            raw = raw_pool.tile([P, 2048], F32, name="raw", tag="raw")
            a_grp[i] = (grp, raw)
            made = banks[("a", i)]
            for b in range(4):
                if b < copies_of(i):
                    words_out(nc.scalar.copy, raw, made[b], b)
                else:
                    nc.scalar.activation(
                        out=grp[:, 1024 * b : 1024 * b + 1024].rearrange(
                            "p (c u e) -> p c u e", u=2, e=2
                        ),
                        in_=made[b][:].bitcast(BF16).rearrange("p u (c e) -> p c u e", e=2),
                        func=ACT.Square,
                    )

        def a_square(i):
            grp, raw = a_grp[i]
            raw_bf = raw[:].bitcast(BF16)
            hi = 1024 * copies_of(i)
            if hi > 0:
                nc.vector.tensor_tensor(
                    out=grp[:, 0:hi], in0=raw_bf[:, 0:hi], in1=raw_bf[:, 0:hi], op=ALU.mult
                )

        def a_quant(i, lo=0, hi=4096):
            if lo == 0:
                a_q[i] = new_codes()
            quantise(a_grp[i][0], a_q[i][0], a_q[i][1], lo, hi)

        units = [[4 * g, 4 * g + 1, 4 * g + 2, 4 * g + 3] for g in range(7)] + [[28, 29, 30], [31]]
        unit_of = {}
        for n, rows in enumerate(units):
            for i in rows:
                unit_of[i] = n
        unit_acc = {}
        unit_ep = {}

        def a_matmuls(i, g_lo=0, g_hi=8):
            n = unit_of[i]
            if i == units[n][0] and g_lo == 0:
                unit_acc[n] = acc_pool.tile([P, 4, OUT_F], F32, name="acc", tag="acc")
            acc = unit_acc[n]
            codes, scales = a_q[i]
            s = i - units[n][0]
            for g in range(g_lo, g_hi):
                cols = slice(128 * g, 128 * g + 128)
                nc.tensor.matmul_mx(
                    out=acc[:, s, :],
                    lhsT=codes[:, cols].bitcast(FP8X4),
                    lhsT_scale=scales[:, cols],
                    rhs=sup_codes[:, cols].bitcast(FP8X4),
                    rhs_scale=sup_scales[:, cols],
                    start=(g == 0),
                    stop=(g == 7),
                )

        bias_f = const.tile([P, OUT_F], F32, name="bias_f")

        def ep_first(n):
            k = len(units[n])
            v = ep_pool.tile([P, 4, OUT_F], F32, name="v", tag="v")
            m = ep_pool.tile([P, 4, OUT_F], F32, name="m", tag="m")
            nc.vector.tensor_tensor(
                out=v[:, 0:k, :],
                in0=unit_acc[n][:, 0:k, :],
                in1=bias_f[:].unsqueeze(1).to_broadcast([P, k, OUT_F]),
                op=ALU.add,
            )
            nc.vector.tensor_scalar_min(out=m[:, 0:k, :], in0=v[:, 0:k, :], scalar1=0.0)
            unit_ep[n] = (v, m)

        def ep_exp(n):
            k = len(units[n])
            v, m = unit_ep[n]
            e = ep_pool.tile([P, 4, OUT_F], F32, name="e", tag="e")
            nc.scalar.activation(out=e[:, 0:k, :], in_=m[:, 0:k, :], func=ACT.Exp)
            unit_ep[n] = (v, e)

        def ep_last(n):
            k = len(units[n])
            v, e = unit_ep[n]
            o = ep_pool.tile([P, 4, OUT_F], F32, name="o", tag="o")
            nc.vector.scalar_tensor_tensor(
                out=o[:, 0:k, :],
                in0=e[:, 0:k, :],
                scalar=-1.0,
                in1=v[:, 0:k, :],
                op0=ALU.add,
                op1=ALU.max,
            )
            first = units[n][0]
            s0 = first % 4
            nc.sync.dma_start(out=out_view[first // 4][:, s0 : s0 + k, :], in_=o[:, 0:k, :])

        transposes(("x", 0))
        for h in range(CHUNKS):
            load_a(A_BUFS - CHUNKS + h)
            if h + 1 < CHUNKS:
                transposes(("x", h + 1))
            else:
                transposes(("a", 0))
                load_a(A_BUFS)
            x_out(h)
            if h > 0:
                sup_out(h - 1)
            x_quant(h)
            x_matmuls(h)
        transposes(("a", 1))
        load_a(A_BUFS + 1)

        first_at = {}
        rest_at = {}

        def multiply(i, at):
            a_matmuls(i)
            n = unit_of[i]
            if i == units[n][-1] and n < len(units) - 2:
                first_at[at + 2] = n
                rest_at[at + 3] = n

        for i in range(TILES - 1):
            if i % 2 == 0:
                for k in (i + 2, i + 3):
                    if 2 <= k < TILES:
                        transposes(("a", k))
                        load_a(k + A_BUFS)
            a_out(i)
            if i in rest_at:
                ep_exp(rest_at[i])
            a_square(i)
            if i == 0:
                sup_out(CHUNKS - 1)
                nc.vector.quantize_mx(
                    out=sup_codes[:].bitcast(FP8X4),
                    scales=sup_scales[:],
                    in_=sup_grp[:].rearrange("p c w t -> p (c w t)"),
                )
            if i == 3:
                nc.vector.tensor_copy(out=bias_f[:], in_=bias_bf[:])
            if i >= 1:
                a_quant(i - 1)
            if i % 2 == 0 and i >= 2:
                multiply(i - 2, i)
                multiply(i - 1, i)
            if i in first_at:
                ep_first(first_at[i])
            if i in rest_at:
                ep_last(rest_at[i])

        assert all([k < TILES - 1 for k in first_at])
        last = TILES - 1
        a_out(last)
        late = [rest_at[k] for k in sorted(rest_at) if k >= last]
        for n in late:
            ep_exp(n)
        a_quant(last - 1)
        a_matmuls(last - 1)
        a_square(last)
        for n in late:
            ep_last(n)
        ep_first(len(units) - 2)
        ep_exp(len(units) - 2)
        cuts = END_CUTS
        for c in range(len(cuts) - 1):
            a_quant(last, cuts[c], cuts[c + 1])
            a_matmuls(last, cuts[c] // 512, cuts[c + 1] // 512)
            if c == 0:
                ep_last(len(units) - 2)
        ep_first(len(units) - 1)
        ep_exp(len(units) - 1)
        ep_last(len(units) - 1)
